import numpy as np
import ml_dtypes


def mxq(x, axis, fmt="e4m3"):
    dtype, down = {"e4m3": (ml_dtypes.float8_e4m3fn, 7), "e5m2": (ml_dtypes.float8_e5m2, 14)}[fmt]
    v = np.moveaxis(np.asarray(x, np.float32).astype(ml_dtypes.bfloat16).astype(np.float64), axis, -1)
    blocks = v.reshape(v.shape[:-1] + (-1, 32))
    amax = np.abs(blocks).max(-1, keepdims=True)
    byte = np.maximum(np.where(amax > 0, np.frexp(amax)[1] - 1 + 127, 0) - down, 1)
    scale = np.exp2(byte - 127.0)
    codes = (blocks / scale).astype(np.float32).astype(dtype).astype(np.float64)
    return np.moveaxis((codes * scale).reshape(v.shape), -1, axis)


WIDE = False


def mx_kscale(k):
    if not WIDE:
        return np.ones(k)
    levels = np.array([10, -10, 5, -5, 0])
    a = np.random.permutation(np.resize(levels, k // 512 * 4)).reshape(k // 512, 4)
    idx = np.arange(k)
    return np.exp2(a[idx // 512, idx % 128 // 32])


BF16 = ml_dtypes.bfloat16


def bf(x):
    return np.asarray(x, np.float32).astype(BF16)


def f64(x):
    return np.asarray(x).astype(np.float64)


E2M1 = np.array([0.0, 0.5, 1.0, 1.5, 2.0, 3.0, 4.0, 6.0, -0.0, -0.5, -1.0, -1.5, -2.0, -3.0, -4.0, -6.0])


def pack_weight(w, fmt):
    k, n = w.shape
    w = f64(bf(w)).reshape(k // 32, 32, n)
    amax = np.abs(w).max(1)
    if fmt == "e4m3":
        byte = np.frexp(amax)[1] - 1 + 127 - 7
    else:
        mant, ex = np.frexp(amax / 6.0)
        byte = np.where(mant > 0.5, ex, ex - 1) + 127
    byte = np.clip(np.where(amax > 0, byte, 1), 1, 254)
    scaled = (w * np.exp2(127.0 - byte)[:, None, :]).reshape(k, n).astype(np.float32)
    by_word = np.ascontiguousarray(scaled.reshape(k // 512, 128, 4, n).transpose(0, 1, 3, 2))
    if fmt == "e4m3":
        words = by_word.astype(ml_dtypes.float8_e4m3fn).view(np.uint8)
    else:
        c = by_word.astype(ml_dtypes.float4_e2m1fn).view(np.uint8) & 0xF
        words = c[..., 0::2] | (c[..., 1::2] << 4)
    return np.ascontiguousarray(words), np.ascontiguousarray(byte.astype(np.uint8).reshape(k // 512, 16, n))


def unpack_weight(words, scales, fmt):
    g, p, n, _ = words.shape
    if fmt == "e4m3":
        vals = np.ascontiguousarray(words).view(ml_dtypes.float8_e4m3fn).astype(np.float64)
    else:
        nib = np.empty((g, p, n, 4), np.uint8)
        nib[..., 0::2] = words & 0xF
        nib[..., 1::2] = words >> 4
        vals = E2M1[nib]
    vals = vals * np.repeat(np.exp2(scales.astype(np.float64) - 127.0), 8, axis=1)[..., None]
    return vals.transpose(0, 1, 3, 2).reshape(g * 512, n)


B, H, W, C, F, KH, KW = 128, 4, 6, 512, 256, 3, 3
OH, OW = H - KH + 1, W - KW + 1
K = KH * KW * C
E = OH * OW
BN_EPS = 1e-3


def extract_patches(x, kh, kw):
    b, h, w, c = x.shape
    oh, ow = h - kh + 1, w - kw + 1
    slices = [x[:, i:i + oh, j:j + ow, :] for i in range(kh) for j in range(kw)]
    return np.stack(slices, axis=3).reshape(b, oh, ow, kh * kw * c)


def setup_inputs():
    s = mx_kscale(C)
    x = bf(np.random.standard_normal((B, H, W, C)) * 0.14)
    gamma = bf((1.0 + 0.1 * np.random.standard_normal(C)) * s)
    beta = bf(0.3 * np.random.standard_normal(C) * s)
    moving_mean = bf(0.05 * np.random.standard_normal(C))
    moving_var = bf(0.01 + 0.02 * np.random.random(C))
    stack = np.random.standard_normal((OH * OW, K, F)) / np.sqrt(K) / np.tile(s, KH * KW)[None, :, None]
    words, scales = pack_weight(stack.reshape(-1, F), "e4m3")
    return {"x": x,
            "gamma": gamma,
            "beta": beta,
            "moving_mean": moving_mean,
            "moving_var": moving_var,
            "weight_words": words,
            "weight_scales": scales}


def reference(x, gamma, beta, moving_mean, moving_var, weight_words, weight_scales):
    inv = f64(gamma) / np.sqrt(f64(moving_var) + BN_EPS)
    xn = (f64(x) - f64(moving_mean)) * inv + f64(beta)
    xq = mxq(xn, 3, "e4m3")
    patches = extract_patches(xq, KH, KW)
    p = patches.reshape(B, OH * OW, K).transpose(1, 0, 2)
    y = p @ unpack_weight(weight_words, weight_scales, "e4m3").reshape(E, K, F)
    y = y.transpose(1, 0, 2).reshape(B, OH, OW, F)
    return np.maximum(y, 0.0)

@@ -1,0 +1,167 @@
+from contextlib import ExitStack
+
+import concourse.mybir as mybir
+from concourse.masks import make_identity
+
+F32 = mybir.dt.float32
+BF16 = mybir.dt.bfloat16
+I32 = mybir.dt.int32
+U32 = mybir.dt.uint32
+U8 = mybir.dt.uint8
+FP8X4 = mybir.dt.float8_e4m3fn_x4
+ACT = mybir.ActivationFunctionType
+ALU = mybir.AluOpType
+
+P = 128
+PACK = 4
+BATCH, HEIGHT, WIDTH, CHANNELS = 128, 4, 6, 512
+KERNEL_H, KERNEL_W = 3, 3
+OUT_H, OUT_W = HEIGHT - KERNEL_H + 1, WIDTH - KERNEL_W + 1
+FEATURES = 256
+BN_EPS = 1e-3
+
+POSITIONS = HEIGHT * WIDTH
+OUTPUTS = OUT_H * OUT_W
+TAPS = KERNEL_H * KERNEL_W
+GROUPS = OUTPUTS * TAPS
+UNIT = 4
+UNITS = POSITIONS // UNIT
+UNIT_COLS = UNIT * BATCH
+WORD_HALVES = 2
+PLANES = 4
+PLANE_COLS = GROUPS // PLANES
+QUADRANTS = 4
+
+FLOPS = 2 * BATCH * OUTPUTS * TAPS * CHANNELS * FEATURES
+
+
+def load_channel_vector(nc, pool, vector, name):
+    tile = pool.tile([P, PACK], BF16, name=name)
+    nc.scalar.dma_start(out=tile[:], in_=vector.rearrange("(p t) -> p t", t=PACK))
+    return tile
+
+
+def tile_blockrf_e_kernel(
+    tc, x, gamma, beta, moving_mean, moving_var, weight_words, weight_scales, out
+):
+    nc = tc.nc
+    with ExitStack() as ctx:
+        ctx.enter_context(tc.manual_schedule())
+        keep = ctx.enter_context(tc.tile_pool(name="keep", bufs=1))
+        stage = ctx.enter_context(tc.tile_pool(name="stage", bufs=3))
+        results = ctx.enter_context(tc.tile_pool(name="results", bufs=4))
+        transposed = ctx.enter_context(tc.psum_pool(name="transposed", bufs=4))
+        sums = ctx.enter_context(tc.psum_pool(name="sums", bufs=4))
+
+        gamma_sb = load_channel_vector(nc, keep, gamma, "gamma_sb")
+        var_sb = load_channel_vector(nc, keep, moving_var, "var_sb")
+        mean_sb = load_channel_vector(nc, keep, moving_mean, "mean_sb")
+        beta_sb = load_channel_vector(nc, keep, beta, "beta_sb")
+
+        x_by_position = x.rearrange("b h w c -> b (h w) c")
+        x_units = []
+        for unit in range(UNITS):
+            x_sb = keep.tile([P, UNIT, CHANNELS], BF16, name="x_sb%d" % unit)
+            nc.sync.dma_start(out=x_sb[:], in_=x_by_position[:, unit * UNIT : (unit + 1) * UNIT, :])
+            x_units.append(x_sb)
+
+        w_planes = keep.tile([P, PLANE_COLS, FEATURES], U8, name="w_planes", align_bytes=64)
+        nc.vector.memset(w_planes[:].bitcast(I32), 0)
+        planes_i32 = w_planes[:].bitcast(I32)
+        scales_i32 = weight_scales.bitcast(I32).rearrange("(col m) q n -> q m col n", m=PLANES)
+        for quadrant in range(QUADRANTS):
+            for r in range(4):
+                first = 32 * quadrant + r
+                nc.sync.dma_start(
+                    out=planes_i32[first : first + 4 * PLANES : 4, :, :],
+                    in_=scales_i32[4 * quadrant + r],
+                )
+
+        words_i32 = (
+            weight_words.rearrange("g p n t -> g p (n t)").bitcast(I32).rearrange("g p n -> p g n")
+        )
+        w_rows = []
+        for row in range(GROUPS // KERNEL_W):
+            w_row = keep.tile([P, KERNEL_W, FEATURES], U32, name="w_row%d" % row, align_bytes=64)
+            nc.sync.dma_start(
+                out=w_row[:].bitcast(I32), in_=words_i32[:, row * KERNEL_W : (row + 1) * KERNEL_W, :]
+            )
+            w_rows.append(w_row)
+
+        identity = keep.tile([P, P], F32, name="identity")
+        make_identity(nc, identity[:])
+
+        var_eps = keep.tile([P, PACK], F32, name="var_eps")
+        nc.vector.tensor_scalar(out=var_eps[:], in0=var_sb[:], scalar1=BN_EPS, scalar2=None, op0=ALU.add)
+        std = keep.tile([P, PACK], F32, name="std")
+        nc.scalar.activation(out=std[:], in_=var_eps[:], func=ACT.Sqrt)
+        rstd0 = keep.tile([P, PACK], F32, name="rstd0")
+        nc.vector.reciprocal(out=rstd0[:], in_=std[:])
+        y_sq = keep.tile([P, PACK], F32, name="y_sq")
+        nc.vector.tensor_tensor(out=y_sq[:], in0=rstd0[:], in1=rstd0[:], op=ALU.mult)
+        a_y_sq = keep.tile([P, PACK], F32, name="a_y_sq")
+        nc.vector.tensor_tensor(out=a_y_sq[:], in0=y_sq[:], in1=var_eps[:], op=ALU.mult)
+        correction = keep.tile([P, PACK], F32, name="correction")
+        nc.vector.tensor_scalar(
+            out=correction[:], in0=a_y_sq[:], scalar1=-0.5, scalar2=1.5, op0=ALU.mult, op1=ALU.add
+        )
+        rstd = keep.tile([P, PACK], F32, name="rstd")
+        nc.vector.tensor_tensor(out=rstd[:], in0=rstd0[:], in1=correction[:], op=ALU.mult)
+        inv = keep.tile([P, PACK], F32, name="inv")
+        nc.vector.tensor_tensor(out=inv[:], in0=gamma_sb[:], in1=rstd[:], op=ALU.mult)
+        mean_inv = keep.tile([P, PACK], F32, name="mean_inv")
+        nc.vector.tensor_tensor(out=mean_inv[:], in0=mean_sb[:], in1=inv[:], op=ALU.mult)
+        shift = keep.tile([P, PACK], F32, name="shift")
+        nc.vector.tensor_tensor(out=shift[:], in0=beta_sb[:], in1=mean_inv[:], op=ALU.subtract)
+
+        x_codes = keep.tile([P, POSITIONS, BATCH], U32, name="x_codes", align_bytes=64)
+        x_planes = keep.tile([P, POSITIONS, BATCH], U8, name="x_planes", align_bytes=64)
+        for unit in range(UNITS):
+            x_words = x_units[unit][:].bitcast(F32)
+            by_channel = stage.tile([P, PACK, UNIT, BATCH], BF16, name="by_channel")
+            for u in range(WORD_HALVES):
+                xt = transposed.tile([P, UNIT, BATCH], F32, name="xt")
+                for j in range(UNIT):
+                    nc.tensor.transpose(xt[:, j, :], x_words[:, j, u :: WORD_HALVES], identity[:])
+                halves = xt[:].bitcast(BF16).rearrange("p j (b e) -> p e j b", e=2)
+                for e in range(2):
+                    t = 2 * u + e
+                    nc.scalar.activation(
+                        out=by_channel[:, t, :, :],
+                        in_=halves[:, e, :, :],
+                        func=ACT.Identity,
+                        scale=inv[:, t : t + 1],
+                        bias=shift[:, t : t + 1],
+                    )
+            grouped = stage.tile([P, UNIT_COLS, PACK], BF16, name="grouped", align_bytes=64)
+            nc.vector.tensor_copy(
+                out=grouped[:].rearrange("p (c i) t -> p c t i", i=4),
+                in_=by_channel[:].rearrange("p t j b -> p t (j b)").rearrange("p t (c i) -> p c t i", i=4),
+            )
+            unit_positions = slice(unit * UNIT, (unit + 1) * UNIT)
+            nc.vector.quantize_mx(
+                out=x_codes[:, unit_positions, :].rearrange("p j b -> p (j b)").bitcast(FP8X4),
+                scales=x_planes[:, unit_positions, :].rearrange("p j b -> p (j b)"),
+                in_=grouped[:].rearrange("p c t -> p (c t)"),
+            )
+
+        out_by_position = out.rearrange("b h w f -> b (h w) f")
+        for e in range(OUTPUTS):
+            h, w = divmod(e, OUT_W)
+            acc = sums.tile([P, FEATURES], F32, name="acc")
+            for tap in range(TAPS):
+                i, j = divmod(tap, KERNEL_W)
+                position = (h + i) * WIDTH + (w + j)
+                col, m = divmod(e * TAPS + tap, PLANES)
+                nc.tensor.matmul_mx(
+                    out=acc[:],
+                    lhsT=x_codes[:, position, :].bitcast(FP8X4),
+                    lhsT_scale=x_planes[:, position, :],
+                    rhs=w_rows[e * KERNEL_H + i][:, j, :].bitcast(FP8X4),
+                    rhs_scale=w_planes[4 * m : P, col, :],
+                    start=(tap == 0),
+                    stop=(tap == TAPS - 1),
+                )
+            y = results.tile([P, FEATURES], F32, name="y")
+            nc.scalar.activation(out=y[:], in_=acc[:], func=ACT.Relu)
+            nc.scalar.dma_start(out=out_by_position[:, e, :], in_=y[:])

@@ -80,13 +80,16 @@ def tile_blockrf_e_kernel(
         words_i32 = (
             weight_words.rearrange("g p n t -> g p (n t)").bitcast(I32).rearrange("g p n -> p g n")
         )
-        w_rows = []
-        for row in range(GROUPS // KERNEL_W):
-            w_row = keep.tile([P, KERNEL_W, FEATURES], U32, name="w_row%d" % row, align_bytes=64)
-            nc.sync.dma_start(
-                out=w_row[:].bitcast(I32), in_=words_i32[:, row * KERNEL_W : (row + 1) * KERNEL_W, :]
-            )
-            w_rows.append(w_row)
+        w_tiles = []
+        for e in range(OUTPUTS):
+            w_tile = keep.tile([P, TAPS, FEATURES], U32, name="w_tile%d" % e, align_bytes=64)
+            step = TAPS if e < OUTPUTS - 1 else KERNEL_W
+            for tap0 in range(0, TAPS, step):
+                nc.sync.dma_start(
+                    out=w_tile[:, tap0 : tap0 + step, :].bitcast(I32),
+                    in_=words_i32[:, e * TAPS + tap0 : e * TAPS + tap0 + step, :],
+                )
+            w_tiles.append(w_tile)
 
         identity = keep.tile([P, P], F32, name="identity")
         make_identity(nc, identity[:])
@@ -157,7 +160,7 @@ def tile_blockrf_e_kernel(
                     out=acc[:],
                     lhsT=x_codes[:, position, :].bitcast(FP8X4),
                     lhsT_scale=x_planes[:, position, :],
-                    rhs=w_rows[e * KERNEL_H + i][:, j, :].bitcast(FP8X4),
+                    rhs=w_tiles[e][:, tap, :].bitcast(FP8X4),
                     rhs_scale=w_planes[4 * m : P, col, :],
                     start=(tap == 0),
                     stop=(tap == TAPS - 1),

@@ -49,7 +49,6 @@ def tile_blockrf_e_kernel(
         ctx.enter_context(tc.manual_schedule())
         keep = ctx.enter_context(tc.tile_pool(name="keep", bufs=1))
         stage = ctx.enter_context(tc.tile_pool(name="stage", bufs=3))
-        results = ctx.enter_context(tc.tile_pool(name="results", bufs=4))
         transposed = ctx.enter_context(tc.psum_pool(name="transposed", bufs=4))
         sums = ctx.enter_context(tc.psum_pool(name="sums", bufs=4))
 
@@ -165,6 +164,7 @@ def tile_blockrf_e_kernel(
                     start=(tap == 0),
                     stop=(tap == TAPS - 1),
                 )
-            y = results.tile([P, FEATURES], F32, name="y")
+            y = keep.tile([P, FEATURES], F32, name="y%d" % e)
             nc.scalar.activation(out=y[:], in_=acc[:], func=ACT.Relu)
-            nc.scalar.dma_start(out=out_by_position[:, e, :], in_=y[:])
+            store_queue = nc.sync if e < OUTPUTS - 1 else nc.scalar
+            store_queue.dma_start(out=out_by_position[:, e, :], in_=y[:])

@@ -57,12 +57,15 @@ def tile_blockrf_e_kernel(
         mean_sb = load_channel_vector(nc, keep, moving_mean, "mean_sb")
         beta_sb = load_channel_vector(nc, keep, beta, "beta_sb")
 
-        x_by_position = x.rearrange("b h w c -> b (h w) c")
         x_units = []
-        for unit in range(UNITS):
-            x_sb = keep.tile([P, UNIT, CHANNELS], BF16, name="x_sb%d" % unit)
-            nc.sync.dma_start(out=x_sb[:], in_=x_by_position[:, unit * UNIT : (unit + 1) * UNIT, :])
-            x_units.append(x_sb)
+        for pair in range(WIDTH // 2):
+            x_sb = keep.tile([P, HEIGHT, 2, CHANNELS], BF16, name="x_sb%d" % pair)
+            nc.sync.dma_start(
+                out=x_sb[:].rearrange("p h w c -> p h (w c)"),
+                in_=x[:, :, 2 * pair : 2 * pair + 2, :].rearrange("b h w c -> b h (w c)"),
+            )
+            for w in range(2):
+                x_units.append(x_sb[:, :, w, :])
 
         w_planes = keep.tile([P, PLANE_COLS, FEATURES], U8, name="w_planes", align_bytes=64)
         nc.vector.memset(w_planes[:].bitcast(I32), 0)
@@ -79,16 +82,21 @@ def tile_blockrf_e_kernel(
         words_i32 = (
             weight_words.rearrange("g p n t -> g p (n t)").bitcast(I32).rearrange("g p n -> p g n")
         )
-        w_tiles = []
-        for e in range(OUTPUTS):
+        e_order = [h * OUT_W + w for w in range(OUT_W) for h in range(OUT_H)]
+        w_tiles = {}
+        for e in e_order:
             w_tile = keep.tile([P, TAPS, FEATURES], U32, name="w_tile%d" % e, align_bytes=64)
-            step = TAPS if e < OUTPUTS - 1 else KERNEL_W
-            for tap0 in range(0, TAPS, step):
+            if e != e_order[-1]:
                 nc.sync.dma_start(
-                    out=w_tile[:, tap0 : tap0 + step, :].bitcast(I32),
-                    in_=words_i32[:, e * TAPS + tap0 : e * TAPS + tap0 + step, :],
+                    out=w_tile[:].bitcast(I32), in_=words_i32[:, e * TAPS : (e + 1) * TAPS, :]
                 )
-            w_tiles.append(w_tile)
+            else:
+                for j in range(KERNEL_W):
+                    nc.sync.dma_start(
+                        out=w_tile[:, j::KERNEL_W, :].bitcast(I32),
+                        in_=words_i32[:, e * TAPS + j : (e + 1) * TAPS : KERNEL_W, :],
+                    )
+            w_tiles[e] = w_tile
 
         identity = keep.tile([P, P], F32, name="identity")
         make_identity(nc, identity[:])
@@ -119,7 +127,7 @@ def tile_blockrf_e_kernel(
         x_codes = keep.tile([P, POSITIONS, BATCH], U32, name="x_codes", align_bytes=64)
         x_planes = keep.tile([P, POSITIONS, BATCH], U8, name="x_planes", align_bytes=64)
         for unit in range(UNITS):
-            x_words = x_units[unit][:].bitcast(F32)
+            x_words = x_units[unit].bitcast(F32)
             by_channel = stage.tile([P, PACK, UNIT, BATCH], BF16, name="by_channel")
             for u in range(WORD_HALVES):
                 xt = transposed.tile([P, UNIT, BATCH], F32, name="xt")
@@ -148,12 +156,13 @@ def tile_blockrf_e_kernel(
             )
 
         out_by_position = out.rearrange("b h w f -> b (h w) f")
-        for e in range(OUTPUTS):
+        taps = [i * KERNEL_W + j for j in range(KERNEL_W) for i in range(KERNEL_H)]
+        for e in e_order:
             h, w = divmod(e, OUT_W)
             acc = sums.tile([P, FEATURES], F32, name="acc")
-            for tap in range(TAPS):
+            for tap in taps:
                 i, j = divmod(tap, KERNEL_W)
-                position = (h + i) * WIDTH + (w + j)
+                position = (w + j) * UNIT + (h + i)
                 col, m = divmod(e * TAPS + tap, PLANES)
                 nc.tensor.matmul_mx(
                     out=acc[:],
@@ -161,10 +170,10 @@ def tile_blockrf_e_kernel(
                     lhsT_scale=x_planes[:, position, :],
                     rhs=w_tiles[e][:, tap, :].bitcast(FP8X4),
                     rhs_scale=w_planes[4 * m : P, col, :],
-                    start=(tap == 0),
-                    stop=(tap == TAPS - 1),
+                    start=(tap == taps[0]),
+                    stop=(tap == taps[-1]),
                 )
             y = keep.tile([P, FEATURES], F32, name="y%d" % e)
             nc.scalar.activation(out=y[:], in_=acc[:], func=ACT.Relu)
-            store_queue = nc.sync if e < OUTPUTS - 1 else nc.scalar
+            store_queue = nc.sync if e != e_order[-1] else nc.scalar
             store_queue.dma_start(out=out_by_position[:, e, :], in_=y[:])

@@ -35,10 +35,8 @@ QUADRANTS = 4
 FLOPS = 2 * BATCH * OUTPUTS * TAPS * CHANNELS * FEATURES
 
 
-def load_channel_vector(nc, pool, vector, name):
-    tile = pool.tile([P, PACK], BF16, name=name)
-    nc.scalar.dma_start(out=tile[:], in_=vector.rearrange("(p t) -> p t", t=PACK))
-    return tile
+LARGE_IN_ROUND = 2
+SCALES_IN_ROUND = 6
 
 
 def tile_blockrf_e_kernel(
@@ -52,17 +50,27 @@ def tile_blockrf_e_kernel(
         transposed = ctx.enter_context(tc.psum_pool(name="transposed", bufs=4))
         sums = ctx.enter_context(tc.psum_pool(name="sums", bufs=4))
 
-        gamma_sb = load_channel_vector(nc, keep, gamma, "gamma_sb")
-        var_sb = load_channel_vector(nc, keep, moving_var, "var_sb")
-        mean_sb = load_channel_vector(nc, keep, moving_mean, "mean_sb")
-        beta_sb = load_channel_vector(nc, keep, beta, "beta_sb")
+        large_loads = []
+        scale_loads = []
+
+        def channel_vector(vector, name):
+            tile = keep.tile([P, PACK], BF16, name=name)
+            nc.scalar.dma_start(out=tile[:], in_=vector.rearrange("(p t) -> p t", t=PACK))
+            return tile
+
+        gamma_sb = channel_vector(gamma, "gamma_sb")
+        var_sb = channel_vector(moving_var, "var_sb")
+        mean_sb = channel_vector(moving_mean, "mean_sb")
+        beta_sb = channel_vector(beta, "beta_sb")
 
         x_units = []
         for pair in range(WIDTH // 2):
             x_sb = keep.tile([P, HEIGHT, 2, CHANNELS], BF16, name="x_sb%d" % pair)
-            nc.sync.dma_start(
-                out=x_sb[:].rearrange("p h w c -> p h (w c)"),
-                in_=x[:, :, 2 * pair : 2 * pair + 2, :].rearrange("b h w c -> b h (w c)"),
+            large_loads.append(
+                (
+                    x_sb[:].rearrange("p h w c -> p h (w c)"),
+                    x[:, :, 2 * pair : 2 * pair + 2, :].rearrange("b h w c -> b h (w c)"),
+                )
             )
             for w in range(2):
                 x_units.append(x_sb[:, :, w, :])
@@ -74,9 +82,8 @@ def tile_blockrf_e_kernel(
         for quadrant in range(QUADRANTS):
             for r in range(4):
                 first = 32 * quadrant + r
-                nc.sync.dma_start(
-                    out=planes_i32[first : first + 4 * PLANES : 4, :, :],
-                    in_=scales_i32[4 * quadrant + r],
+                scale_loads.append(
+                    (planes_i32[first : first + 4 * PLANES : 4, :, :], scales_i32[4 * quadrant + r])
                 )
 
         words_i32 = (
@@ -87,16 +94,23 @@ def tile_blockrf_e_kernel(
         for e in e_order:
             w_tile = keep.tile([P, TAPS, FEATURES], U32, name="w_tile%d" % e, align_bytes=64)
             if e != e_order[-1]:
-                nc.sync.dma_start(
-                    out=w_tile[:].bitcast(I32), in_=words_i32[:, e * TAPS : (e + 1) * TAPS, :]
-                )
+                large_loads.append((w_tile[:].bitcast(I32), words_i32[:, e * TAPS : (e + 1) * TAPS, :]))
             else:
                 for j in range(KERNEL_W):
-                    nc.sync.dma_start(
-                        out=w_tile[:, j::KERNEL_W, :].bitcast(I32),
-                        in_=words_i32[:, e * TAPS + j : (e + 1) * TAPS : KERNEL_W, :],
+                    large_loads.append(
+                        (
+                            w_tile[:, j::KERNEL_W, :].bitcast(I32),
+                            words_i32[:, e * TAPS + j : (e + 1) * TAPS : KERNEL_W, :],
+                        )
                     )
             w_tiles[e] = w_tile
+
+        rounds = (len(large_loads) + LARGE_IN_ROUND - 1) // LARGE_IN_ROUND
+        for n in range(rounds):
+            for out_ap, in_ap in large_loads[n * LARGE_IN_ROUND : (n + 1) * LARGE_IN_ROUND]:
+                nc.sync.dma_start(out=out_ap, in_=in_ap)
+            for out_ap, in_ap in scale_loads[n * SCALES_IN_ROUND : (n + 1) * SCALES_IN_ROUND]:
+                nc.sync.dma_start(out=out_ap, in_=in_ap)
 
         identity = keep.tile([P, P], F32, name="identity")
         make_identity(nc, identity[:])

@@ -35,8 +35,7 @@ QUADRANTS = 4
 FLOPS = 2 * BATCH * OUTPUTS * TAPS * CHANNELS * FEATURES
 
 
-LARGE_IN_ROUND = 2
-SCALES_IN_ROUND = 6
+ROUNDS = ((2, 6), (1, 6), (1, 4))
 
 
 def tile_blockrf_e_kernel(
@@ -105,12 +104,13 @@ def tile_blockrf_e_kernel(
                     )
             w_tiles[e] = w_tile
 
-        rounds = (len(large_loads) + LARGE_IN_ROUND - 1) // LARGE_IN_ROUND
-        for n in range(rounds):
-            for out_ap, in_ap in large_loads[n * LARGE_IN_ROUND : (n + 1) * LARGE_IN_ROUND]:
+        for large, small in ROUNDS:
+            for out_ap, in_ap in large_loads[:large] + scale_loads[:small]:
                 nc.sync.dma_start(out=out_ap, in_=in_ap)
-            for out_ap, in_ap in scale_loads[n * SCALES_IN_ROUND : (n + 1) * SCALES_IN_ROUND]:
-                nc.sync.dma_start(out=out_ap, in_=in_ap)
+            large_loads = large_loads[large:]
+            scale_loads = scale_loads[small:]
+        for out_ap, in_ap in large_loads:
+            nc.sync.dma_start(out=out_ap, in_=in_ap)
 
         identity = keep.tile([P, P], F32, name="identity")
         make_identity(nc, identity[:])

@@ -54,7 +54,7 @@ def tile_blockrf_e_kernel(
 
         def channel_vector(vector, name):
             tile = keep.tile([P, PACK], BF16, name=name)
-            nc.scalar.dma_start(out=tile[:], in_=vector.rearrange("(p t) -> p t", t=PACK))
+            nc.sync.dma_start(out=tile[:], in_=vector.rearrange("(p t) -> p t", t=PACK))
             return tile
 
         gamma_sb = channel_vector(gamma, "gamma_sb")

@@ -35,7 +35,7 @@ QUADRANTS = 4
 FLOPS = 2 * BATCH * OUTPUTS * TAPS * CHANNELS * FEATURES
 
 
-ROUNDS = ((2, 6), (1, 6), (1, 4))
+ROUNDS = ((1, 3), (1, 3), (1, 3), (1, 3), (1, 4))
 
 
 def tile_blockrf_e_kernel(

@@ -30,6 +30,8 @@ UNIT_COLS = UNIT * BATCH
 WORD_HALVES = 2
 PLANES = 4
 PLANE_COLS = GROUPS // PLANES
+STORES = ((0, 2), (4, 2), (2, 2), (6, 1), (7, 1))
+LAST_LOADS = (4, 3, 2)
 QUADRANTS = 4
 
 FLOPS = 2 * BATCH * OUTPUTS * TAPS * CHANNELS * FEATURES
@@ -78,8 +80,8 @@ def tile_blockrf_e_kernel(
         nc.vector.memset(w_planes[:].bitcast(I32), 0)
         planes_i32 = w_planes[:].bitcast(I32)
         scales_i32 = weight_scales.bitcast(I32).rearrange("(col m) q n -> q m col n", m=PLANES)
-        for quadrant in range(QUADRANTS):
-            for r in range(4):
+        for r in range(4):
+            for quadrant in (0, 2, 1, 3):
                 first = 32 * quadrant + r
                 scale_loads.append(
                     (planes_i32[first : first + 4 * PLANES : 4, :, :], scales_i32[4 * quadrant + r])
@@ -95,13 +97,15 @@ def tile_blockrf_e_kernel(
             if e != e_order[-1]:
                 large_loads.append((w_tile[:].bitcast(I32), words_i32[:, e * TAPS : (e + 1) * TAPS, :]))
             else:
-                for j in range(KERNEL_W):
+                first = 0
+                for count in LAST_LOADS:
                     large_loads.append(
                         (
-                            w_tile[:, j::KERNEL_W, :].bitcast(I32),
-                            words_i32[:, e * TAPS + j : (e + 1) * TAPS : KERNEL_W, :],
+                            w_tile[:, first : first + count, :].bitcast(I32),
+                            words_i32[:, e * TAPS + first : e * TAPS + first + count, :],
                         )
                     )
+                    first += count
             w_tiles[e] = w_tile
 
         for large, small in ROUNDS:
@@ -170,8 +174,14 @@ def tile_blockrf_e_kernel(
             )
 
         out_by_position = out.rearrange("b h w f -> b (h w) f")
-        taps = [i * KERNEL_W + j for j in range(KERNEL_W) for i in range(KERNEL_H)]
+        store_of = {}
+        for first, positions in STORES:
+            for e in range(first, first + positions):
+                store_of[e] = (first, positions)
+        y_tiles = {}
+        by_column = [i * KERNEL_W + j for j in range(KERNEL_W) for i in range(KERNEL_H)]
         for e in e_order:
+            taps = by_column if e != e_order[-1] else list(range(TAPS))
             h, w = divmod(e, OUT_W)
             acc = sums.tile([P, FEATURES], F32, name="acc")
             for tap in taps:
@@ -187,7 +197,11 @@ def tile_blockrf_e_kernel(
                     start=(tap == taps[0]),
                     stop=(tap == taps[-1]),
                 )
-            y = keep.tile([P, FEATURES], F32, name="y%d" % e)
-            nc.scalar.activation(out=y[:], in_=acc[:], func=ACT.Relu)
-            store_queue = nc.sync if e != e_order[-1] else nc.scalar
-            store_queue.dma_start(out=out_by_position[:, e, :], in_=y[:])
+            first, positions = store_of[e]
+            if first not in y_tiles:
+                y_tiles[first] = keep.tile([P, positions, FEATURES], F32, name="y%d" % first)
+            y = y_tiles[first]
+            nc.scalar.activation(out=y[:, e - first, :], in_=acc[:], func=ACT.Relu)
+            if e == first + positions - 1:
+                store_queue = nc.sync if e != e_order[-1] else nc.scalar
+                store_queue.dma_start(out=out_by_position[:, first : first + positions, :], in_=y[:])

from contextlib import ExitStack

import concourse.mybir as mybir
from concourse.masks import make_identity

F32 = mybir.dt.float32
BF16 = mybir.dt.bfloat16
I32 = mybir.dt.int32
U32 = mybir.dt.uint32
U8 = mybir.dt.uint8
FP8X4 = mybir.dt.float8_e4m3fn_x4
ACT = mybir.ActivationFunctionType
ALU = mybir.AluOpType

P = 128
PACK = 4
BATCH, HEIGHT, WIDTH, CHANNELS = 128, 4, 6, 512
KERNEL_H, KERNEL_W = 3, 3
OUT_H, OUT_W = HEIGHT - KERNEL_H + 1, WIDTH - KERNEL_W + 1
FEATURES = 256
BN_EPS = 1e-3

POSITIONS = HEIGHT * WIDTH
OUTPUTS = OUT_H * OUT_W
TAPS = KERNEL_H * KERNEL_W
GROUPS = OUTPUTS * TAPS
UNIT = 4
UNITS = POSITIONS // UNIT
UNIT_COLS = UNIT * BATCH
WORD_HALVES = 2
PLANES = 4
PLANE_COLS = GROUPS // PLANES
STORES = ((0, 2), (4, 2), (2, 2), (6, 1), (7, 1))
LAST_LOADS = (4, 3, 2)
QUADRANTS = 4

FLOPS = 2 * BATCH * OUTPUTS * TAPS * CHANNELS * FEATURES


ROUNDS = ((1, 3), (1, 3), (1, 3), (1, 3), (1, 4))


def tile_blockrf_e_kernel(
    tc, x, gamma, beta, moving_mean, moving_var, weight_words, weight_scales, out
):
    nc = tc.nc
    with ExitStack() as ctx:
        ctx.enter_context(tc.manual_schedule())
        keep = ctx.enter_context(tc.tile_pool(name="keep", bufs=1))
        stage = ctx.enter_context(tc.tile_pool(name="stage", bufs=3))
        transposed = ctx.enter_context(tc.psum_pool(name="transposed", bufs=4))
        sums = ctx.enter_context(tc.psum_pool(name="sums", bufs=4))

        large_loads = []
        scale_loads = []

        def channel_vector(vector, name):
            tile = keep.tile([P, PACK], BF16, name=name)
            nc.sync.dma_start(out=tile[:], in_=vector.rearrange("(p t) -> p t", t=PACK))
            return tile

        gamma_sb = channel_vector(gamma, "gamma_sb")
        var_sb = channel_vector(moving_var, "var_sb")
        mean_sb = channel_vector(moving_mean, "mean_sb")
        beta_sb = channel_vector(beta, "beta_sb")

        x_units = []
        for pair in range(WIDTH // 2):
            x_sb = keep.tile([P, HEIGHT, 2, CHANNELS], BF16, name="x_sb%d" % pair)
            large_loads.append(
                (
                    x_sb[:].rearrange("p h w c -> p h (w c)"),
                    x[:, :, 2 * pair : 2 * pair + 2, :].rearrange("b h w c -> b h (w c)"),
                )
            )
            for w in range(2):
                x_units.append(x_sb[:, :, w, :])

        w_planes = keep.tile([P, PLANE_COLS, FEATURES], U8, name="w_planes", align_bytes=64)
        nc.vector.memset(w_planes[:].bitcast(I32), 0)
        planes_i32 = w_planes[:].bitcast(I32)
        scales_i32 = weight_scales.bitcast(I32).rearrange("(col m) q n -> q m col n", m=PLANES)
        for r in range(4):
            for quadrant in (0, 2, 1, 3):
                first = 32 * quadrant + r
                scale_loads.append(
                    (planes_i32[first : first + 4 * PLANES : 4, :, :], scales_i32[4 * quadrant + r])
                )

        words_i32 = (
            weight_words.rearrange("g p n t -> g p (n t)").bitcast(I32).rearrange("g p n -> p g n")
        )
        e_order = [h * OUT_W + w for w in range(OUT_W) for h in range(OUT_H)]
        w_tiles = {}
        for e in e_order:
            w_tile = keep.tile([P, TAPS, FEATURES], U32, name="w_tile%d" % e, align_bytes=64)
            if e != e_order[-1]:
                large_loads.append((w_tile[:].bitcast(I32), words_i32[:, e * TAPS : (e + 1) * TAPS, :]))
            else:
                first = 0
                for count in LAST_LOADS:
                    large_loads.append(
                        (
                            w_tile[:, first : first + count, :].bitcast(I32),
                            words_i32[:, e * TAPS + first : e * TAPS + first + count, :],
                        )
                    )
                    first += count
            w_tiles[e] = w_tile

        for large, small in ROUNDS:
            for out_ap, in_ap in large_loads[:large] + scale_loads[:small]:
                nc.sync.dma_start(out=out_ap, in_=in_ap)
            large_loads = large_loads[large:]
            scale_loads = scale_loads[small:]
        for out_ap, in_ap in large_loads:
            nc.sync.dma_start(out=out_ap, in_=in_ap)

        identity = keep.tile([P, P], F32, name="identity")
        make_identity(nc, identity[:])

        var_eps = keep.tile([P, PACK], F32, name="var_eps")
        nc.vector.tensor_scalar(out=var_eps[:], in0=var_sb[:], scalar1=BN_EPS, scalar2=None, op0=ALU.add)
        std = keep.tile([P, PACK], F32, name="std")
        nc.scalar.activation(out=std[:], in_=var_eps[:], func=ACT.Sqrt)
        rstd0 = keep.tile([P, PACK], F32, name="rstd0")
        nc.vector.reciprocal(out=rstd0[:], in_=std[:])
        y_sq = keep.tile([P, PACK], F32, name="y_sq")
        nc.vector.tensor_tensor(out=y_sq[:], in0=rstd0[:], in1=rstd0[:], op=ALU.mult)
        a_y_sq = keep.tile([P, PACK], F32, name="a_y_sq")
        nc.vector.tensor_tensor(out=a_y_sq[:], in0=y_sq[:], in1=var_eps[:], op=ALU.mult)
        correction = keep.tile([P, PACK], F32, name="correction")
        nc.vector.tensor_scalar(
            out=correction[:], in0=a_y_sq[:], scalar1=-0.5, scalar2=1.5, op0=ALU.mult, op1=ALU.add
        )
        rstd = keep.tile([P, PACK], F32, name="rstd")
        nc.vector.tensor_tensor(out=rstd[:], in0=rstd0[:], in1=correction[:], op=ALU.mult)
        inv = keep.tile([P, PACK], F32, name="inv")
        nc.vector.tensor_tensor(out=inv[:], in0=gamma_sb[:], in1=rstd[:], op=ALU.mult)
        mean_inv = keep.tile([P, PACK], F32, name="mean_inv")
        nc.vector.tensor_tensor(out=mean_inv[:], in0=mean_sb[:], in1=inv[:], op=ALU.mult)
        shift = keep.tile([P, PACK], F32, name="shift")
        nc.vector.tensor_tensor(out=shift[:], in0=beta_sb[:], in1=mean_inv[:], op=ALU.subtract)

        x_codes = keep.tile([P, POSITIONS, BATCH], U32, name="x_codes", align_bytes=64)
        x_planes = keep.tile([P, POSITIONS, BATCH], U8, name="x_planes", align_bytes=64)
        for unit in range(UNITS):
            x_words = x_units[unit].bitcast(F32)
            by_channel = stage.tile([P, PACK, UNIT, BATCH], BF16, name="by_channel")
            for u in range(WORD_HALVES):
                xt = transposed.tile([P, UNIT, BATCH], F32, name="xt")
                for j in range(UNIT):
                    nc.tensor.transpose(xt[:, j, :], x_words[:, j, u :: WORD_HALVES], identity[:])
                halves = xt[:].bitcast(BF16).rearrange("p j (b e) -> p e j b", e=2)
                for e in range(2):
                    t = 2 * u + e
                    nc.scalar.activation(
                        out=by_channel[:, t, :, :],
                        in_=halves[:, e, :, :],
                        func=ACT.Identity,
                        scale=inv[:, t : t + 1],
                        bias=shift[:, t : t + 1],
                    )
            grouped = stage.tile([P, UNIT_COLS, PACK], BF16, name="grouped", align_bytes=64)
            nc.vector.tensor_copy(
                out=grouped[:].rearrange("p (c i) t -> p c t i", i=4),
                in_=by_channel[:].rearrange("p t j b -> p t (j b)").rearrange("p t (c i) -> p c t i", i=4),
            )
            unit_positions = slice(unit * UNIT, (unit + 1) * UNIT)
            nc.vector.quantize_mx(
                out=x_codes[:, unit_positions, :].rearrange("p j b -> p (j b)").bitcast(FP8X4),
                scales=x_planes[:, unit_positions, :].rearrange("p j b -> p (j b)"),
                in_=grouped[:].rearrange("p c t -> p (c t)"),
            )

        out_by_position = out.rearrange("b h w f -> b (h w) f")
        store_of = {}
        for first, positions in STORES:
            for e in range(first, first + positions):
                store_of[e] = (first, positions)
        y_tiles = {}
        by_column = [i * KERNEL_W + j for j in range(KERNEL_W) for i in range(KERNEL_H)]
        for e in e_order:
            taps = by_column if e != e_order[-1] else list(range(TAPS))
            h, w = divmod(e, OUT_W)
            acc = sums.tile([P, FEATURES], F32, name="acc")
            for tap in taps:
                i, j = divmod(tap, KERNEL_W)
                position = (w + j) * UNIT + (h + i)
                col, m = divmod(e * TAPS + tap, PLANES)
                nc.tensor.matmul_mx(
                    out=acc[:],
                    lhsT=x_codes[:, position, :].bitcast(FP8X4),
                    lhsT_scale=x_planes[:, position, :],
                    rhs=w_tiles[e][:, tap, :].bitcast(FP8X4),
                    rhs_scale=w_planes[4 * m : P, col, :],
                    start=(tap == taps[0]),
                    stop=(tap == taps[-1]),
                )
            first, positions = store_of[e]
            if first not in y_tiles:
                y_tiles[first] = keep.tile([P, positions, FEATURES], F32, name="y%d" % first)
            y = y_tiles[first]
            nc.scalar.activation(out=y[:, e - first, :], in_=acc[:], func=ACT.Relu)
            if e == first + positions - 1:
                store_queue = nc.sync if e != e_order[-1] else nc.scalar
                store_queue.dma_start(out=out_by_position[:, first : first + positions, :], in_=y[:])
